import numpy as np
import ml_dtypes

BF16 = ml_dtypes.bfloat16


def bf(x):
    return np.asarray(x, np.float32).astype(BF16)


def f32(x):
    return np.asarray(x, np.float32)


def f64(x):
    return np.asarray(x).astype(np.float64)


def striped(idx):
    return np.tile(idx.reshape(-1, 16).T, (8, 1))


C, S, N, O, K, Q = 512, 2048, 2048, 1024, 16, 4
T = f64((np.arange(K)[:, None] >> (Q - 1 - np.arange(Q))[None, :]) & 1)


def setup_inputs():
    return {"x": f32(np.random.uniform(size=(C, S))), "weights": f32(np.random.standard_normal((K, O))), "offs": striped(np.random.permutation(np.tile(np.arange(S), 2))[:N])}


def reference(x, weights, offs):
    idx = offs[:16].T.reshape(-1)
    picked = f64(x)[:, idx]
    a, b = picked[:, :O], picked[:, O:]
    e = np.exp(f64(weights))
    p = e / e.sum(axis=0, keepdims=True)
    m = T.T @ p
    na, nb = 1.0 - a, 1.0 - b
    return m[0] * na * nb + m[1] * na * b + m[2] * a * nb + m[3] * a * b

@@ -1,0 +1,107 @@
+import concourse.mybir as mybir
+from concourse.masks import make_identity
+
+F32 = mybir.dt.float32
+U16 = mybir.dt.uint16
+ALU = mybir.AluOpType
+ACT = mybir.ActivationFunctionType
+AXIS = mybir.AxisListType
+
+P = 128
+SAMPLES, SIGNALS = 512, 2048
+KINDS, GATES = 16, 1024
+CHUNKS = GATES // P
+BANK = 512
+HALVES = GATES // BANK
+ONE, B, A, AB = 0, 1, 2, 3
+
+
+def tile_logiclayer_kernel(tc, x, weights, offs, out):
+    nc = tc.nc
+    with (
+        tc.tile_pool(name="held", bufs=1) as held,
+        tc.tile_pool(name="windows", bufs=SAMPLES // P) as windows,
+        tc.tile_pool(name="gathered", bufs=2) as gathered,
+        tc.tile_pool(name="work", bufs=2) as work,
+        tc.psum_pool(name="banks", bufs=8) as banks,
+    ):
+        offsets = held.tile([P, (2 * GATES) // 16], U16, name="offsets")
+        nc.sync.dma_start(offsets[:], offs)
+
+        w_rows = held.tile([P, P], F32, name="w_rows")
+        nc.sync.dma_start(w_rows[:], weights.rearrange("k (c j) -> (k c) j", c=CHUNKS))
+        identity = held.tile([P, P], F32, name="identity")
+        make_identity(nc, identity[:])
+
+        w_cols = banks.tile([P, BANK], F32, name="w_cols", tag="bank")
+        nc.tensor.transpose(w_cols[:, 0:P], w_rows[:], identity[:])
+        by_kind = w_cols[:, 0:P].rearrange("j (k c) -> j k c", c=CHUNKS)
+
+        top = held.tile([P, CHUNKS], F32, name="top")
+        nc.vector.tensor_reduce(
+            top[:], w_cols[:, 0:P].rearrange("j (k c) -> j c k", c=CHUNKS), AXIS.X, ALU.max
+        )
+        e = held.tile([P, KINDS * CHUNKS], F32, name="e")
+        e_by_kind = e[:].rearrange("j (k c) -> j k c", c=CHUNKS)
+        nc.vector.tensor_tensor(
+            e_by_kind, by_kind, top[:].unsqueeze(1).to_broadcast([P, KINDS, CHUNKS]), ALU.subtract
+        )
+        nc.scalar.activation(e[:], e[:], ACT.Exp)
+
+        total = held.tile([P, CHUNKS], F32, name="total")
+        nc.vector.tensor_reduce(
+            total[:], e[:].rearrange("j (k c) -> j c k", c=CHUNKS), AXIS.X, ALU.add
+        )
+        coef = held.tile([P, 4, CHUNKS], F32, name="coef")
+        for q in range(4):
+            bit_set = e[:].rearrange(
+                "j (h b l c) -> j b c h l", h=2**q, b=2, l=2 ** (3 - q), c=CHUNKS
+            )[:, 1]
+            nc.vector.tensor_reduce(coef[:, q, :], bit_set, AXIS.XY, ALU.add)
+        nc.vector.reciprocal(total[:], total[:])
+        nc.vector.tensor_mul(coef[:], coef[:], total[:].unsqueeze(1).to_broadcast([P, 4, CHUNKS]))
+        nc.vector.tensor_sub(coef[:, AB, :], coef[:, AB, :], coef[:, A, :])
+        nc.vector.tensor_sub(
+            coef[:, B : A + 1, :],
+            coef[:, B : A + 1, :],
+            coef[:, ONE : ONE + 1, :].to_broadcast([P, 2, CHUNKS]),
+        )
+        nc.vector.tensor_sub(coef[:, AB, :], coef[:, AB, :], coef[:, B, :])
+
+        spread = {}
+        for q in (AB, B, A, ONE):
+            for half in range(HALVES):
+                bank = banks.tile([P, BANK], F32, name=f"spread{q}_{half}", tag="bank")
+                for c in range(BANK // P):
+                    chunk = half * (BANK // P) + c
+                    nc.tensor.transpose(
+                        bank[:, c * P : (c + 1) * P],
+                        coef[:, q, chunk : chunk + 1].to_broadcast([P, P]),
+                        identity[:],
+                    )
+                spread[q, half] = bank
+
+        for blk in range(SAMPLES // P):
+            rows = slice(blk * P, (blk + 1) * P)
+            window = windows.tile([P, SIGNALS], F32, name="window")
+            nc.sync.dma_start(window[:], x[rows, :])
+            picked = gathered.tile([P, 2 * GATES], F32, name="picked")
+            for side in range(2):
+                nc.scalar.activation(
+                    picked[:, side * GATES : (side + 1) * GATES],
+                    window[:].indirect(offsets[:, side * (GATES // 16) : (side + 1) * (GATES // 16)]),
+                    ACT.Copy,
+                )
+            result = work.tile([P, GATES], F32, name="result")
+            for half in range(HALVES):
+                a = picked[:, half * BANK : (half + 1) * BANK]
+                b = picked[:, GATES + half * BANK : GATES + (half + 1) * BANK]
+                slope = work.tile([P, BANK], F32, name="slope")
+                nc.vector.tensor_mul(slope[:], a, spread[AB, half][:])
+                nc.vector.tensor_add(slope[:], slope[:], spread[B, half][:])
+                nc.vector.tensor_mul(slope[:], slope[:], b)
+                base = work.tile([P, BANK], F32, name="base")
+                nc.vector.tensor_mul(base[:], a, spread[A, half][:])
+                nc.vector.tensor_add(base[:], base[:], spread[ONE, half][:])
+                nc.vector.tensor_add(result[:, half * BANK : (half + 1) * BANK], slope[:], base[:])
+            nc.sync.dma_start(out[rows, :], result[:])

@@ -9,10 +9,14 @@ AXIS = mybir.AxisListType
 
 P = 128
 SAMPLES, SIGNALS = 512, 2048
+BLOCKS = SAMPLES // P
 KINDS, GATES = 16, 1024
 CHUNKS = GATES // P
 BANK = 512
+PER_BANK = BANK // P
 HALVES = GATES // BANK
+UNITS = BLOCKS * HALVES
+LEAD = 2
 ONE, B, A, AB = 0, 1, 2, 3
 
 
@@ -20,44 +24,43 @@ def tile_logiclayer_kernel(tc, x, weights, offs, out):
     nc = tc.nc
     with (
         tc.tile_pool(name="held", bufs=1) as held,
-        tc.tile_pool(name="windows", bufs=SAMPLES // P) as windows,
-        tc.tile_pool(name="gathered", bufs=2) as gathered,
-        tc.tile_pool(name="work", bufs=2) as work,
-        tc.psum_pool(name="banks", bufs=8) as banks,
+        tc.tile_pool(name="windows", bufs=BLOCKS) as windows,
+        tc.tile_pool(name="work", bufs=3) as work,
+        tc.psum_pool(name="flips", bufs=2) as flips,
+        tc.psum_pool(name="backs", bufs=LEAD + 1) as backs,
     ):
-        offsets = held.tile([P, (2 * GATES) // 16], U16, name="offsets")
-        nc.sync.dma_start(offsets[:], offs)
-
         w_rows = held.tile([P, P], F32, name="w_rows")
         nc.sync.dma_start(w_rows[:], weights.rearrange("k (c j) -> (k c) j", c=CHUNKS))
+        offsets = held.tile([P, (2 * GATES) // 16], U16, name="offsets")
+        nc.sync.dma_start(offsets[:], offs)
         identity = held.tile([P, P], F32, name="identity")
         make_identity(nc, identity[:])
-
-        w_cols = banks.tile([P, BANK], F32, name="w_cols", tag="bank")
-        nc.tensor.transpose(w_cols[:, 0:P], w_rows[:], identity[:])
-        by_kind = w_cols[:, 0:P].rearrange("j (k c) -> j k c", c=CHUNKS)
-
-        top = held.tile([P, CHUNKS], F32, name="top")
-        nc.vector.tensor_reduce(
-            top[:], w_cols[:, 0:P].rearrange("j (k c) -> j c k", c=CHUNKS), AXIS.X, ALU.max
-        )
-        e = held.tile([P, KINDS * CHUNKS], F32, name="e")
-        e_by_kind = e[:].rearrange("j (k c) -> j k c", c=CHUNKS)
-        nc.vector.tensor_tensor(
-            e_by_kind, by_kind, top[:].unsqueeze(1).to_broadcast([P, KINDS, CHUNKS]), ALU.subtract
-        )
-        nc.scalar.activation(e[:], e[:], ACT.Exp)
-
-        total = held.tile([P, CHUNKS], F32, name="total")
-        nc.vector.tensor_reduce(
-            total[:], e[:].rearrange("j (k c) -> j c k", c=CHUNKS), AXIS.X, ALU.add
-        )
         coef = held.tile([P, 4, CHUNKS], F32, name="coef")
-        for q in range(4):
-            bit_set = e[:].rearrange(
-                "j (h b l c) -> j b c h l", h=2**q, b=2, l=2 ** (3 - q), c=CHUNKS
-            )[:, 1]
-            nc.vector.tensor_reduce(coef[:, q, :], bit_set, AXIS.XY, ALU.add)
+        total = held.tile([P, CHUNKS], F32, name="total")
+
+        w_cols = flips.tile([P, BANK], F32, name="w_cols", tag="flipped")
+        nc.tensor.transpose(w_cols[:, 0:P], w_rows[:], identity[:])
+        with tc.tile_pool(name="softmax", bufs=1) as softmax:
+            top = softmax.tile([P, CHUNKS], F32, name="top")
+            nc.vector.tensor_reduce(
+                top[:], w_cols[:, 0:P].rearrange("j (k c) -> j c k", c=CHUNKS), AXIS.X, ALU.max
+            )
+            e = softmax.tile([P, KINDS * CHUNKS], F32, name="e")
+            nc.vector.tensor_tensor(
+                e[:].rearrange("j (k c) -> j k c", c=CHUNKS),
+                w_cols[:, 0:P].rearrange("j (k c) -> j k c", c=CHUNKS),
+                top[:].unsqueeze(1).to_broadcast([P, KINDS, CHUNKS]),
+                ALU.subtract,
+            )
+            nc.scalar.activation(e[:], e[:], ACT.Exp)
+            nc.vector.tensor_reduce(
+                total[:], e[:].rearrange("j (k c) -> j c k", c=CHUNKS), AXIS.X, ALU.add
+            )
+            for q in range(4):
+                bit_set = e[:].rearrange(
+                    "j (h b l c) -> j b c h l", h=2**q, b=2, l=2 ** (3 - q), c=CHUNKS
+                )[:, 1]
+                nc.vector.tensor_reduce(coef[:, q, :], bit_set, AXIS.XY, ALU.add)
         nc.vector.reciprocal(total[:], total[:])
         nc.vector.tensor_mul(coef[:], coef[:], total[:].unsqueeze(1).to_broadcast([P, 4, CHUNKS]))
         nc.vector.tensor_sub(coef[:, AB, :], coef[:, AB, :], coef[:, A, :])
@@ -68,40 +71,68 @@ def tile_logiclayer_kernel(tc, x, weights, offs, out):
         )
         nc.vector.tensor_sub(coef[:, AB, :], coef[:, AB, :], coef[:, B, :])
 
-        spread = {}
-        for q in (AB, B, A, ONE):
-            for half in range(HALVES):
-                bank = banks.tile([P, BANK], F32, name=f"spread{q}_{half}", tag="bank")
-                for c in range(BANK // P):
-                    chunk = half * (BANK // P) + c
-                    nc.tensor.transpose(
-                        bank[:, c * P : (c + 1) * P],
-                        coef[:, q, chunk : chunk + 1].to_broadcast([P, P]),
-                        identity[:],
-                    )
-                spread[q, half] = bank
+        with tc.tile_pool(name="gathered", bufs=BLOCKS) as gathered:
+            window, picked = [], []
+            for blk in range(BLOCKS):
+                window.append(windows.tile([P, SIGNALS], F32, name="window"))
+                nc.sync.dma_start(window[blk][:], x[blk * P : (blk + 1) * P, :])
+                picked.append(gathered.tile([P, 2 * GATES], F32, name="picked"))
 
-        for blk in range(SAMPLES // P):
-            rows = slice(blk * P, (blk + 1) * P)
-            window = windows.tile([P, SIGNALS], F32, name="window")
-            nc.sync.dma_start(window[:], x[rows, :])
-            picked = gathered.tile([P, 2 * GATES], F32, name="picked")
-            for side in range(2):
+            def gather(unit, side):
+                blk, half = divmod(unit, HALVES)
+                first = side * GATES + half * BANK
                 nc.scalar.activation(
-                    picked[:, side * GATES : (side + 1) * GATES],
-                    window[:].indirect(offsets[:, side * (GATES // 16) : (side + 1) * (GATES // 16)]),
+                    picked[blk][:, first : first + BANK],
+                    window[blk][:].indirect(offsets[:, first // 16 : (first + BANK) // 16]),
                     ACT.Copy,
                 )
-            result = work.tile([P, GATES], F32, name="result")
-            for half in range(HALVES):
-                a = picked[:, half * BANK : (half + 1) * BANK]
-                b = picked[:, GATES + half * BANK : GATES + (half + 1) * BANK]
-                slope = work.tile([P, BANK], F32, name="slope")
-                nc.vector.tensor_mul(slope[:], a, spread[AB, half][:])
-                nc.vector.tensor_add(slope[:], slope[:], spread[B, half][:])
-                nc.vector.tensor_mul(slope[:], slope[:], b)
-                base = work.tile([P, BANK], F32, name="base")
-                nc.vector.tensor_mul(base[:], a, spread[A, half][:])
-                nc.vector.tensor_add(base[:], base[:], spread[ONE, half][:])
-                nc.vector.tensor_add(result[:, half * BANK : (half + 1) * BANK], slope[:], base[:])
-            nc.sync.dma_start(out[rows, :], result[:])
+                return picked[blk][:, first : first + BANK]
+
+            def slope_and_base(unit):
+                a = gather(unit, 0)
+                half = unit % HALVES
+                spans = [slice(c * P, (c + 1) * P) for c in range(PER_BANK)]
+                a_flipped = flips.tile([P, BANK], F32, name="a_flipped", tag="flipped")
+                for span in spans:
+                    nc.tensor.transpose(a_flipped[:, span], a[:, span], identity[:])
+                slope_flipped = work.tile([P, BANK], F32, name="slope_flipped")
+                base_flipped = work.tile([P, BANK], F32, name="base_flipped")
+                for c, span in enumerate(spans):
+                    chunk = half * PER_BANK + c
+                    nc.vector.tensor_scalar(
+                        slope_flipped[:, span],
+                        a_flipped[:, span],
+                        coef[:, AB, chunk : chunk + 1],
+                        coef[:, B, chunk : chunk + 1],
+                        ALU.mult,
+                        ALU.add,
+                    )
+                    nc.vector.tensor_scalar(
+                        base_flipped[:, span],
+                        a_flipped[:, span],
+                        coef[:, A, chunk : chunk + 1],
+                        coef[:, ONE, chunk : chunk + 1],
+                        ALU.mult,
+                        ALU.add,
+                    )
+                slope = backs.tile([P, BANK], F32, name="slope")
+                base = backs.tile([P, BANK], F32, name="base")
+                for span in spans:
+                    nc.tensor.transpose(slope[:, span], slope_flipped[:, span], identity[:])
+                for span in spans:
+                    nc.tensor.transpose(base[:, span], base_flipped[:, span], identity[:])
+                return slope, base
+
+            ready = [slope_and_base(unit) for unit in range(LEAD)]
+            for unit in range(UNITS):
+                if unit + LEAD < UNITS:
+                    ready.append(slope_and_base(unit + LEAD))
+                b = gather(unit, 1)
+                slope, base = ready[unit]
+                result = work.tile([P, BANK], F32, name="result")
+                nc.vector.tensor_mul(result[:], b, slope[:])
+                nc.vector.tensor_add(result[:], result[:], base[:])
+                blk, half = divmod(unit, HALVES)
+                nc.sync.dma_start(
+                    out[blk * P : (blk + 1) * P, half * BANK : (half + 1) * BANK], result[:]
+                )

@@ -37,6 +37,7 @@ def tile_logiclayer_kernel(tc, x, weights, offs, out):
         make_identity(nc, identity[:])
         coef = held.tile([P, 4, CHUNKS], F32, name="coef")
         total = held.tile([P, CHUNKS], F32, name="total")
+        e = held.tile([P, KINDS * CHUNKS], F32, name="e")
 
         w_cols = flips.tile([P, BANK], F32, name="w_cols", tag="flipped")
         nc.tensor.transpose(w_cols[:, 0:P], w_rows[:], identity[:])
@@ -45,22 +46,22 @@ def tile_logiclayer_kernel(tc, x, weights, offs, out):
             nc.vector.tensor_reduce(
                 top[:], w_cols[:, 0:P].rearrange("j (k c) -> j c k", c=CHUNKS), AXIS.X, ALU.max
             )
-            e = softmax.tile([P, KINDS * CHUNKS], F32, name="e")
+            shifted = softmax.tile([P, KINDS * CHUNKS], F32, name="shifted")
             nc.vector.tensor_tensor(
-                e[:].rearrange("j (k c) -> j k c", c=CHUNKS),
+                shifted[:].rearrange("j (k c) -> j k c", c=CHUNKS),
                 w_cols[:, 0:P].rearrange("j (k c) -> j k c", c=CHUNKS),
                 top[:].unsqueeze(1).to_broadcast([P, KINDS, CHUNKS]),
                 ALU.subtract,
             )
-            nc.scalar.activation(e[:], e[:], ACT.Exp)
-            nc.vector.tensor_reduce(
-                total[:], e[:].rearrange("j (k c) -> j c k", c=CHUNKS), AXIS.X, ALU.add
-            )
-            for q in range(4):
-                bit_set = e[:].rearrange(
-                    "j (h b l c) -> j b c h l", h=2**q, b=2, l=2 ** (3 - q), c=CHUNKS
-                )[:, 1]
-                nc.vector.tensor_reduce(coef[:, q, :], bit_set, AXIS.XY, ALU.add)
+            nc.scalar.activation(e[:], shifted[:], ACT.Exp)
+        nc.vector.tensor_reduce(
+            total[:], e[:].rearrange("j (k c) -> j c k", c=CHUNKS), AXIS.X, ALU.add
+        )
+        for q in range(4):
+            bit_set = e[:].rearrange(
+                "j (h b l c) -> j b c h l", h=2**q, b=2, l=2 ** (3 - q), c=CHUNKS
+            )[:, 1]
+            nc.vector.tensor_reduce(coef[:, q, :], bit_set, AXIS.XY, ALU.add)
         nc.vector.reciprocal(total[:], total[:])
         nc.vector.tensor_mul(coef[:], coef[:], total[:].unsqueeze(1).to_broadcast([P, 4, CHUNKS]))
         nc.vector.tensor_sub(coef[:, AB, :], coef[:, AB, :], coef[:, A, :])

@@ -16,7 +16,8 @@ BANK = 512
 PER_BANK = BANK // P
 HALVES = GATES // BANK
 UNITS = BLOCKS * HALVES
-LEAD = 2
+BACK_LEAD = 2
+FLIP_LEAD = 3
 ONE, B, A, AB = 0, 1, 2, 3
 
 
@@ -27,7 +28,7 @@ def tile_logiclayer_kernel(tc, x, weights, offs, out):
         tc.tile_pool(name="windows", bufs=BLOCKS) as windows,
         tc.tile_pool(name="work", bufs=3) as work,
         tc.psum_pool(name="flips", bufs=2) as flips,
-        tc.psum_pool(name="backs", bufs=LEAD + 1) as backs,
+        tc.psum_pool(name="backs", bufs=BACK_LEAD + 1) as backs,
     ):
         w_rows = held.tile([P, P], F32, name="w_rows")
         nc.sync.dma_start(w_rows[:], weights.rearrange("k (c j) -> (k c) j", c=CHUNKS))
@@ -89,13 +90,17 @@ def tile_logiclayer_kernel(tc, x, weights, offs, out):
                 )
                 return picked[blk][:, first : first + BANK]
 
-            def slope_and_base(unit):
+            spans = [slice(c * P, (c + 1) * P) for c in range(PER_BANK)]
+
+            def flip_a(unit):
                 a = gather(unit, 0)
-                half = unit % HALVES
-                spans = [slice(c * P, (c + 1) * P) for c in range(PER_BANK)]
                 a_flipped = flips.tile([P, BANK], F32, name="a_flipped", tag="flipped")
                 for span in spans:
                     nc.tensor.transpose(a_flipped[:, span], a[:, span], identity[:])
+                return a_flipped
+
+            def slope_and_base(unit, a_flipped):
+                half = unit % HALVES
                 slope_flipped = work.tile([P, BANK], F32, name="slope_flipped")
                 base_flipped = work.tile([P, BANK], F32, name="base_flipped")
                 for c, span in enumerate(spans):
@@ -124,12 +129,8 @@ def tile_logiclayer_kernel(tc, x, weights, offs, out):
                     nc.tensor.transpose(base[:, span], base_flipped[:, span], identity[:])
                 return slope, base
 
-            ready = [slope_and_base(unit) for unit in range(LEAD)]
-            for unit in range(UNITS):
-                if unit + LEAD < UNITS:
-                    ready.append(slope_and_base(unit + LEAD))
+            def finish(unit, slope, base):
                 b = gather(unit, 1)
-                slope, base = ready[unit]
                 result = work.tile([P, BANK], F32, name="result")
                 nc.vector.tensor_mul(result[:], b, slope[:])
                 nc.vector.tensor_add(result[:], result[:], base[:])
@@ -137,3 +138,14 @@ def tile_logiclayer_kernel(tc, x, weights, offs, out):
                 nc.sync.dma_start(
                     out[blk * P : (blk + 1) * P, half * BANK : (half + 1) * BANK], result[:]
                 )
+
+            flipped, ready = {}, {}
+            for step in range(-FLIP_LEAD, UNITS):
+                if 0 <= step + FLIP_LEAD < UNITS:
+                    flipped[step + FLIP_LEAD] = flip_a(step + FLIP_LEAD)
+                if 0 <= step + BACK_LEAD < UNITS:
+                    ready[step + BACK_LEAD] = slope_and_base(
+                        step + BACK_LEAD, flipped[step + BACK_LEAD]
+                    )
+                if step >= 0:
+                    finish(step, *ready[step])

@@ -129,10 +129,13 @@ def tile_logiclayer_kernel(tc, x, weights, offs, out):
                     nc.tensor.transpose(base[:, span], base_flipped[:, span], identity[:])
                 return slope, base
 
-            def finish(unit, slope, base):
+            def times_b(unit, slope):
                 b = gather(unit, 1)
                 result = work.tile([P, BANK], F32, name="result")
                 nc.vector.tensor_mul(result[:], b, slope[:])
+                return result
+
+            def finish(unit, result, base):
                 nc.vector.tensor_add(result[:], result[:], base[:])
                 blk, half = divmod(unit, HALVES)
                 nc.sync.dma_start(
@@ -141,6 +144,9 @@ def tile_logiclayer_kernel(tc, x, weights, offs, out):
 
             flipped, ready = {}, {}
             for step in range(-FLIP_LEAD, UNITS):
+                if step >= 0:
+                    slope, base = ready[step]
+                    result = times_b(step, slope)
                 if 0 <= step + FLIP_LEAD < UNITS:
                     flipped[step + FLIP_LEAD] = flip_a(step + FLIP_LEAD)
                 if 0 <= step + BACK_LEAD < UNITS:
@@ -148,4 +154,4 @@ def tile_logiclayer_kernel(tc, x, weights, offs, out):
                         step + BACK_LEAD, flipped[step + BACK_LEAD]
                     )
                 if step >= 0:
-                    finish(step, *ready[step])
+                    finish(step, result, base)

@@ -142,8 +142,26 @@ def tile_logiclayer_kernel(tc, x, weights, offs, out):
                     out[blk * P : (blk + 1) * P, half * BANK : (half + 1) * BANK], result[:]
                 )
 
+            def last_b_side(unit, slope, base):
+                blk, half = divmod(unit, HALVES)
+                result = work.tile([P, BANK], F32, name="result")
+                for part in (slice(0, BANK // 2), slice(BANK // 2, BANK)):
+                    first = GATES + half * BANK + part.start
+                    b = picked[blk][:, first : first + BANK // 2]
+                    nc.scalar.activation(
+                        b,
+                        window[blk][:].indirect(offsets[:, first // 16 : (first + BANK // 2) // 16]),
+                        ACT.Copy,
+                    )
+                    nc.vector.tensor_mul(result[:, part], b, slope[:, part])
+                    nc.vector.tensor_add(result[:, part], result[:, part], base[:, part])
+                    nc.sync.dma_start(
+                        out[blk * P : (blk + 1) * P, half * BANK : (half + 1) * BANK][:, part],
+                        result[:, part],
+                    )
+
             flipped, ready = {}, {}
-            for step in range(-FLIP_LEAD, UNITS):
+            for step in range(-FLIP_LEAD, UNITS - 1):
                 if step >= 0:
                     slope, base = ready[step]
                     result = times_b(step, slope)
@@ -155,3 +173,4 @@ def tile_logiclayer_kernel(tc, x, weights, offs, out):
                     )
                 if step >= 0:
                     finish(step, result, base)
+            last_b_side(UNITS - 1, *ready[UNITS - 1])

@@ -18,6 +18,7 @@ HALVES = GATES // BANK
 UNITS = BLOCKS * HALVES
 BACK_LEAD = 2
 FLIP_LEAD = 3
+GPSIMD_HALF = 1
 ONE, B, A, AB = 0, 1, 2, 3
 
 
@@ -27,6 +28,7 @@ def tile_logiclayer_kernel(tc, x, weights, offs, out):
         tc.tile_pool(name="held", bufs=1) as held,
         tc.tile_pool(name="windows", bufs=BLOCKS) as windows,
         tc.tile_pool(name="work", bufs=3) as work,
+        tc.tile_pool(name="results", bufs=UNITS) as results,
         tc.psum_pool(name="flips", bufs=2) as flips,
         tc.psum_pool(name="backs", bufs=BACK_LEAD + 1) as backs,
     ):
@@ -73,6 +75,20 @@ def tile_logiclayer_kernel(tc, x, weights, offs, out):
         )
         nc.vector.tensor_sub(coef[:, AB, :], coef[:, AB, :], coef[:, B, :])
 
+        spread = held.tile([P, 2, BANK], F32, name="spread")
+
+        def spread_coefficients():
+            for row, (q, bank) in enumerate(((A, "slope"), (ONE, "base"))):
+                repeated = backs.tile([P, BANK], F32, name="repeated", tag=bank)
+                for c in range(PER_BANK):
+                    chunk = GPSIMD_HALF * PER_BANK + c
+                    nc.tensor.transpose(
+                        repeated[:, c * P : (c + 1) * P],
+                        coef[:, q, chunk : chunk + 1].to_broadcast([P, P]),
+                        identity[:],
+                    )
+                nc.vector.tensor_copy(spread[:, row, :], repeated[:])
+
         with tc.tile_pool(name="gathered", bufs=BLOCKS) as gathered:
             window, picked = [], []
             for blk in range(BLOCKS):
@@ -99,10 +115,23 @@ def tile_logiclayer_kernel(tc, x, weights, offs, out):
                     nc.tensor.transpose(a_flipped[:, span], a[:, span], identity[:])
                 return a_flipped
 
+            def on_gpsimd(unit):
+                return unit % HALVES == GPSIMD_HALF and unit < UNITS - 1
+
+            def base_on_gpsimd(unit):
+                blk, half = divmod(unit, HALVES)
+                a = picked[blk][:, half * BANK : (half + 1) * BANK]
+                base = work.tile([P, BANK], F32, name="base_rows")
+                nc.gpsimd.tensor_tensor(base[:], a, spread[:, 0, :], ALU.mult)
+                nc.gpsimd.tensor_tensor(base[:], base[:], spread[:, 1, :], ALU.add)
+                return base
+
             def slope_and_base(unit, a_flipped):
                 half = unit % HALVES
                 slope_flipped = work.tile([P, BANK], F32, name="slope_flipped")
-                base_flipped = work.tile([P, BANK], F32, name="base_flipped")
+                both = not on_gpsimd(unit)
+                if both:
+                    base_flipped = work.tile([P, BANK], F32, name="base_flipped")
                 for c, span in enumerate(spans):
                     chunk = half * PER_BANK + c
                     nc.vector.tensor_scalar(
@@ -113,30 +142,37 @@ def tile_logiclayer_kernel(tc, x, weights, offs, out):
                         ALU.mult,
                         ALU.add,
                     )
-                    nc.vector.tensor_scalar(
-                        base_flipped[:, span],
-                        a_flipped[:, span],
-                        coef[:, A, chunk : chunk + 1],
-                        coef[:, ONE, chunk : chunk + 1],
-                        ALU.mult,
-                        ALU.add,
-                    )
+                    if both:
+                        nc.vector.tensor_scalar(
+                            base_flipped[:, span],
+                            a_flipped[:, span],
+                            coef[:, A, chunk : chunk + 1],
+                            coef[:, ONE, chunk : chunk + 1],
+                            ALU.mult,
+                            ALU.add,
+                        )
+                return slope_flipped, base_flipped if both else None
+
+            def flip_back(unit, slope_flipped, base_flipped):
                 slope = backs.tile([P, BANK], F32, name="slope")
-                base = backs.tile([P, BANK], F32, name="base")
                 for span in spans:
                     nc.tensor.transpose(slope[:, span], slope_flipped[:, span], identity[:])
+                if base_flipped is None:
+                    return slope, base_on_gpsimd(unit)
+                base = backs.tile([P, BANK], F32, name="base")
                 for span in spans:
                     nc.tensor.transpose(base[:, span], base_flipped[:, span], identity[:])
                 return slope, base
 
             def times_b(unit, slope):
                 b = gather(unit, 1)
-                result = work.tile([P, BANK], F32, name="result")
+                result = results.tile([P, BANK], F32, name="result")
                 nc.vector.tensor_mul(result[:], b, slope[:])
                 return result
 
             def finish(unit, result, base):
-                nc.vector.tensor_add(result[:], result[:], base[:])
+                adder = nc.gpsimd if on_gpsimd(unit) else nc.vector
+                adder.tensor_tensor(result[:], result[:], base[:], ALU.add)
                 blk, half = divmod(unit, HALVES)
                 nc.sync.dma_start(
                     out[blk * P : (blk + 1) * P, half * BANK : (half + 1) * BANK], result[:]
@@ -144,7 +180,7 @@ def tile_logiclayer_kernel(tc, x, weights, offs, out):
 
             def last_b_side(unit, slope, base):
                 blk, half = divmod(unit, HALVES)
-                result = work.tile([P, BANK], F32, name="result")
+                result = results.tile([P, BANK], F32, name="result")
                 for part in (slice(0, BANK // 2), slice(BANK // 2, BANK)):
                     first = GATES + half * BANK + part.start
                     b = picked[blk][:, first : first + BANK // 2]
@@ -160,17 +196,19 @@ def tile_logiclayer_kernel(tc, x, weights, offs, out):
                         result[:, part],
                     )
 
-            flipped, ready = {}, {}
+            flipped, made, ready = {}, {}, {}
             for step in range(-FLIP_LEAD, UNITS - 1):
+                if 0 <= step + BACK_LEAD < UNITS:
+                    made[step + BACK_LEAD] = slope_and_base(
+                        step + BACK_LEAD, flipped[step + BACK_LEAD]
+                    )
+                if step == -BACK_LEAD:
+                    spread_coefficients()
                 if step >= 0:
                     slope, base = ready[step]
-                    result = times_b(step, slope)
+                    finish(step, times_b(step, slope), base)
                 if 0 <= step + FLIP_LEAD < UNITS:
                     flipped[step + FLIP_LEAD] = flip_a(step + FLIP_LEAD)
                 if 0 <= step + BACK_LEAD < UNITS:
-                    ready[step + BACK_LEAD] = slope_and_base(
-                        step + BACK_LEAD, flipped[step + BACK_LEAD]
-                    )
-                if step >= 0:
-                    finish(step, result, base)
+                    ready[step + BACK_LEAD] = flip_back(step + BACK_LEAD, *made[step + BACK_LEAD])
             last_b_side(UNITS - 1, *ready[UNITS - 1])

@@ -16,9 +16,8 @@ BANK = 512
 PER_BANK = BANK // P
 HALVES = GATES // BANK
 UNITS = BLOCKS * HALVES
-BACK_LEAD = 2
-FLIP_LEAD = 3
-GPSIMD_HALF = 1
+A_LEAD = 2
+GPSIMD_HALF = 0
 ONE, B, A, AB = 0, 1, 2, 3
 
 
@@ -27,10 +26,11 @@ def tile_logiclayer_kernel(tc, x, weights, offs, out):
     with (
         tc.tile_pool(name="held", bufs=1) as held,
         tc.tile_pool(name="windows", bufs=BLOCKS) as windows,
-        tc.tile_pool(name="work", bufs=3) as work,
-        tc.tile_pool(name="results", bufs=UNITS) as results,
-        tc.psum_pool(name="flips", bufs=2) as flips,
-        tc.psum_pool(name="backs", bufs=BACK_LEAD + 1) as backs,
+        tc.tile_pool(name="work", bufs=(A_LEAD + 1) * HALVES) as work,
+        tc.tile_pool(name="results", bufs=UNITS) as results_pool,
+        tc.psum_pool(name="flips", bufs=3) as flips,
+        tc.psum_pool(name="slopes", bufs=3) as slopes,
+        tc.psum_pool(name="bases", bufs=2) as bases,
     ):
         w_rows = held.tile([P, P], F32, name="w_rows")
         nc.sync.dma_start(w_rows[:], weights.rearrange("k (c j) -> (k c) j", c=CHUNKS))
@@ -78,8 +78,8 @@ def tile_logiclayer_kernel(tc, x, weights, offs, out):
         spread = held.tile([P, 2, BANK], F32, name="spread")
 
         def spread_coefficients():
-            for row, (q, bank) in enumerate(((A, "slope"), (ONE, "base"))):
-                repeated = backs.tile([P, BANK], F32, name="repeated", tag=bank)
+            for row, q in enumerate((A, ONE)):
+                repeated = slopes.tile([P, BANK], F32, name="repeated", tag="slope")
                 for c in range(PER_BANK):
                     chunk = GPSIMD_HALF * PER_BANK + c
                     nc.tensor.transpose(
@@ -89,38 +89,40 @@ def tile_logiclayer_kernel(tc, x, weights, offs, out):
                     )
                 nc.vector.tensor_copy(spread[:, row, :], repeated[:])
 
-        with tc.tile_pool(name="gathered", bufs=BLOCKS) as gathered:
-            window, picked = [], []
+        with tc.tile_pool(name="gathered", bufs=3) as gathered:
+            window, picked = [], {}
             for blk in range(BLOCKS):
                 window.append(windows.tile([P, SIGNALS], F32, name="window"))
                 nc.sync.dma_start(window[blk][:], x[blk * P : (blk + 1) * P, :])
-                picked.append(gathered.tile([P, 2 * GATES], F32, name="picked"))
 
-            def gather(unit, side):
-                blk, half = divmod(unit, HALVES)
-                first = side * GATES + half * BANK
+            def gather(blk, side, start, count):
+                if start == 0:
+                    picked[blk, side] = gathered.tile([P, GATES], F32, name="picked")
+                first = side * GATES + start
                 nc.scalar.activation(
-                    picked[blk][:, first : first + BANK],
-                    window[blk][:].indirect(offsets[:, first // 16 : (first + BANK) // 16]),
+                    picked[blk, side][:, start : start + count],
+                    window[blk][:].indirect(offsets[:, first // 16 : (first + count) // 16]),
                     ACT.Copy,
                 )
-                return picked[blk][:, first : first + BANK]
+
+            def part_of_picked(unit, side):
+                blk, half = divmod(unit, HALVES)
+                return picked[blk, side][:, half * BANK : (half + 1) * BANK]
 
             spans = [slice(c * P, (c + 1) * P) for c in range(PER_BANK)]
 
             def flip_a(unit):
-                a = gather(unit, 0)
+                a = part_of_picked(unit, 0)
                 a_flipped = flips.tile([P, BANK], F32, name="a_flipped", tag="flipped")
                 for span in spans:
                     nc.tensor.transpose(a_flipped[:, span], a[:, span], identity[:])
                 return a_flipped
 
             def on_gpsimd(unit):
-                return unit % HALVES == GPSIMD_HALF and unit < UNITS - 1
+                return unit % HALVES == GPSIMD_HALF and unit >= HALVES
 
             def base_on_gpsimd(unit):
-                blk, half = divmod(unit, HALVES)
-                a = picked[blk][:, half * BANK : (half + 1) * BANK]
+                a = part_of_picked(unit, 0)
                 base = work.tile([P, BANK], F32, name="base_rows")
                 nc.gpsimd.tensor_tensor(base[:], a, spread[:, 0, :], ALU.mult)
                 nc.gpsimd.tensor_tensor(base[:], base[:], spread[:, 1, :], ALU.add)
@@ -154,61 +156,78 @@ def tile_logiclayer_kernel(tc, x, weights, offs, out):
                 return slope_flipped, base_flipped if both else None
 
             def flip_back(unit, slope_flipped, base_flipped):
-                slope = backs.tile([P, BANK], F32, name="slope")
+                slope = slopes.tile([P, BANK], F32, name="slope")
                 for span in spans:
                     nc.tensor.transpose(slope[:, span], slope_flipped[:, span], identity[:])
                 if base_flipped is None:
                     return slope, base_on_gpsimd(unit)
-                base = backs.tile([P, BANK], F32, name="base")
+                base = bases.tile([P, BANK], F32, name="base")
                 for span in spans:
                     nc.tensor.transpose(base[:, span], base_flipped[:, span], identity[:])
                 return slope, base
 
-            def times_b(unit, slope):
-                b = gather(unit, 1)
-                result = results.tile([P, BANK], F32, name="result")
-                nc.vector.tensor_mul(result[:], b, slope[:])
-                return result
+            def times_b(unit, slope, result, part):
+                b = part_of_picked(unit, 1)
+                nc.vector.tensor_mul(result[:, part], b[:, part], slope[:, part])
 
-            def finish(unit, result, base):
+            def plus_base(unit, result, base, part):
                 adder = nc.gpsimd if on_gpsimd(unit) else nc.vector
-                adder.tensor_tensor(result[:], result[:], base[:], ALU.add)
-                blk, half = divmod(unit, HALVES)
-                nc.sync.dma_start(
-                    out[blk * P : (blk + 1) * P, half * BANK : (half + 1) * BANK], result[:]
-                )
+                adder.tensor_tensor(result[:, part], result[:, part], base[:, part], ALU.add)
 
-            def last_b_side(unit, slope, base):
+            def store(unit, result, part):
                 blk, half = divmod(unit, HALVES)
-                result = results.tile([P, BANK], F32, name="result")
+                rows = out[blk * P : (blk + 1) * P, half * BANK : (half + 1) * BANK]
+                nc.sync.dma_start(rows[:, part], result[:, part])
+
+            whole = slice(0, BANK)
+            ready = {}
+
+            def units_of(blk):
+                return range(blk * HALVES, (blk + 1) * HALVES)
+
+            def flips_of(blk):
+                gather(blk, 0, 0, GATES)
+                return {unit: flip_a(unit) for unit in units_of(blk)}
+
+            def b_side(blk, pieces):
+                units = units_of(blk)
+                results = {unit: results_pool.tile([P, BANK], F32, name="result") for unit in units}
+                for piece in range(pieces):
+                    gather(blk, 1, piece * GATES // pieces, GATES // pieces)
+                for unit in units:
+                    times_b(unit, ready[unit][0], results[unit], whole)
+                for unit in units:
+                    plus_base(unit, results[unit], ready[unit][1], whole)
+                for unit in reversed(units):
+                    store(unit, results[unit], whole)
+
+            def last_b_side(blk):
+                first, last = units_of(blk)
+                result = results_pool.tile([P, BANK], F32, name="result")
+                gather(blk, 1, 0, BANK)
+                times_b(first, ready[first][0], result, whole)
+                plus_base(first, result, ready[first][1], whole)
+                result_last = results_pool.tile([P, BANK], F32, name="result")
                 for part in (slice(0, BANK // 2), slice(BANK // 2, BANK)):
-                    first = GATES + half * BANK + part.start
-                    b = picked[blk][:, first : first + BANK // 2]
-                    nc.scalar.activation(
-                        b,
-                        window[blk][:].indirect(offsets[:, first // 16 : (first + BANK // 2) // 16]),
-                        ACT.Copy,
-                    )
-                    nc.vector.tensor_mul(result[:, part], b, slope[:, part])
-                    nc.vector.tensor_add(result[:, part], result[:, part], base[:, part])
-                    nc.sync.dma_start(
-                        out[blk * P : (blk + 1) * P, half * BANK : (half + 1) * BANK][:, part],
-                        result[:, part],
-                    )
+                    gather(blk, 1, BANK + part.start, BANK // 2)
+                    times_b(last, ready[last][0], result_last, part)
+                    plus_base(last, result_last, ready[last][1], part)
+                    store(last, result_last, part)
+                    if part.start == 0:
+                        store(first, result, whole)
 
-            flipped, made, ready = {}, {}, {}
-            for step in range(-FLIP_LEAD, UNITS - 1):
-                if 0 <= step + BACK_LEAD < UNITS:
-                    made[step + BACK_LEAD] = slope_and_base(
-                        step + BACK_LEAD, flipped[step + BACK_LEAD]
-                    )
-                if step == -BACK_LEAD:
-                    spread_coefficients()
+            spread_coefficients()
+            made = {}
+            for step in range(-A_LEAD, BLOCKS):
+                ahead = step + A_LEAD
+                if ahead < BLOCKS:
+                    flipped = flips_of(ahead)
                 if step >= 0:
-                    slope, base = ready[step]
-                    finish(step, times_b(step, slope), base)
-                if 0 <= step + FLIP_LEAD < UNITS:
-                    flipped[step + FLIP_LEAD] = flip_a(step + FLIP_LEAD)
-                if 0 <= step + BACK_LEAD < UNITS:
-                    ready[step + BACK_LEAD] = flip_back(step + BACK_LEAD, *made[step + BACK_LEAD])
-            last_b_side(UNITS - 1, *ready[UNITS - 1])
+                    for unit in units_of(step):
+                        ready[unit] = flip_back(unit, *made[unit])
+                if ahead < BLOCKS:
+                    for unit, a_flipped in flipped.items():
+                        made[unit] = slope_and_base(unit, a_flipped)
+                if 0 <= step < BLOCKS - 1:
+                    b_side(step, pieces=HALVES if step == BLOCKS - 2 else 1)
+            last_b_side(BLOCKS - 1)

@@ -57,23 +57,23 @@ def tile_logiclayer_kernel(tc, x, weights, offs, out):
                 ALU.subtract,
             )
             nc.scalar.activation(e[:], shifted[:], ACT.Exp)
-        nc.vector.tensor_reduce(
-            total[:], e[:].rearrange("j (k c) -> j c k", c=CHUNKS), AXIS.X, ALU.add
-        )
         for q in range(4):
             bit_set = e[:].rearrange(
                 "j (h b l c) -> j b c h l", h=2**q, b=2, l=2 ** (3 - q), c=CHUNKS
             )[:, 1]
             nc.vector.tensor_reduce(coef[:, q, :], bit_set, AXIS.XY, ALU.add)
-        nc.vector.reciprocal(total[:], total[:])
-        nc.vector.tensor_mul(coef[:], coef[:], total[:].unsqueeze(1).to_broadcast([P, 4, CHUNKS]))
+        nc.vector.tensor_reduce(
+            total[:], e[:].rearrange("j (k c) -> j c k", c=CHUNKS), AXIS.X, ALU.add
+        )
         nc.vector.tensor_sub(coef[:, AB, :], coef[:, AB, :], coef[:, A, :])
         nc.vector.tensor_sub(
             coef[:, B : A + 1, :],
             coef[:, B : A + 1, :],
             coef[:, ONE : ONE + 1, :].to_broadcast([P, 2, CHUNKS]),
         )
+        nc.vector.reciprocal(total[:], total[:])
         nc.vector.tensor_sub(coef[:, AB, :], coef[:, AB, :], coef[:, B, :])
+        nc.vector.tensor_mul(coef[:], coef[:], total[:].unsqueeze(1).to_broadcast([P, 4, CHUNKS]))
 
         spread = held.tile([P, 2, BANK], F32, name="spread")
 
@@ -202,19 +202,13 @@ def tile_logiclayer_kernel(tc, x, weights, offs, out):
                     store(unit, results[unit], whole)
 
             def last_b_side(blk):
-                first, last = units_of(blk)
-                result = results_pool.tile([P, BANK], F32, name="result")
-                gather(blk, 1, 0, BANK)
-                times_b(first, ready[first][0], result, whole)
-                plus_base(first, result, ready[first][1], whole)
-                result_last = results_pool.tile([P, BANK], F32, name="result")
-                for part in (slice(0, BANK // 2), slice(BANK // 2, BANK)):
-                    gather(blk, 1, BANK + part.start, BANK // 2)
-                    times_b(last, ready[last][0], result_last, part)
-                    plus_base(last, result_last, ready[last][1], part)
-                    store(last, result_last, part)
-                    if part.start == 0:
-                        store(first, result, whole)
+                for unit in units_of(blk):
+                    result = results_pool.tile([P, BANK], F32, name="result")
+                    for part in (slice(0, BANK // 2), slice(BANK // 2, BANK)):
+                        gather(blk, 1, unit % HALVES * BANK + part.start, BANK // 2)
+                        times_b(unit, ready[unit][0], result, part)
+                        plus_base(unit, result, ready[unit][1], part)
+                        store(unit, result, part)
 
             spread_coefficients()
             made = {}

import concourse.mybir as mybir
from concourse.masks import make_identity

F32 = mybir.dt.float32
U16 = mybir.dt.uint16
ALU = mybir.AluOpType
ACT = mybir.ActivationFunctionType
AXIS = mybir.AxisListType

P = 128
SAMPLES, SIGNALS = 512, 2048
BLOCKS = SAMPLES // P
KINDS, GATES = 16, 1024
CHUNKS = GATES // P
BANK = 512
PER_BANK = BANK // P
HALVES = GATES // BANK
UNITS = BLOCKS * HALVES
A_LEAD = 2
GPSIMD_HALF = 0
ONE, B, A, AB = 0, 1, 2, 3


def tile_logiclayer_kernel(tc, x, weights, offs, out):
    nc = tc.nc
    with (
        tc.tile_pool(name="held", bufs=1) as held,
        tc.tile_pool(name="windows", bufs=BLOCKS) as windows,
        tc.tile_pool(name="work", bufs=(A_LEAD + 1) * HALVES) as work,
        tc.tile_pool(name="results", bufs=UNITS) as results_pool,
        tc.psum_pool(name="flips", bufs=3) as flips,
        tc.psum_pool(name="slopes", bufs=3) as slopes,
        tc.psum_pool(name="bases", bufs=2) as bases,
    ):
        w_rows = held.tile([P, P], F32, name="w_rows")
        nc.sync.dma_start(w_rows[:], weights.rearrange("k (c j) -> (k c) j", c=CHUNKS))
        offsets = held.tile([P, (2 * GATES) // 16], U16, name="offsets")
        nc.sync.dma_start(offsets[:], offs)
        identity = held.tile([P, P], F32, name="identity")
        make_identity(nc, identity[:])
        coef = held.tile([P, 4, CHUNKS], F32, name="coef")
        total = held.tile([P, CHUNKS], F32, name="total")
        e = held.tile([P, KINDS * CHUNKS], F32, name="e")

        w_cols = flips.tile([P, BANK], F32, name="w_cols", tag="flipped")
        nc.tensor.transpose(w_cols[:, 0:P], w_rows[:], identity[:])
        with tc.tile_pool(name="softmax", bufs=1) as softmax:
            top = softmax.tile([P, CHUNKS], F32, name="top")
            nc.vector.tensor_reduce(
                top[:], w_cols[:, 0:P].rearrange("j (k c) -> j c k", c=CHUNKS), AXIS.X, ALU.max
            )
            shifted = softmax.tile([P, KINDS * CHUNKS], F32, name="shifted")
            nc.vector.tensor_tensor(
                shifted[:].rearrange("j (k c) -> j k c", c=CHUNKS),
                w_cols[:, 0:P].rearrange("j (k c) -> j k c", c=CHUNKS),
                top[:].unsqueeze(1).to_broadcast([P, KINDS, CHUNKS]),
                ALU.subtract,
            )
            nc.scalar.activation(e[:], shifted[:], ACT.Exp)
        for q in range(4):
            bit_set = e[:].rearrange(
                "j (h b l c) -> j b c h l", h=2**q, b=2, l=2 ** (3 - q), c=CHUNKS
            )[:, 1]
            nc.vector.tensor_reduce(coef[:, q, :], bit_set, AXIS.XY, ALU.add)
        nc.vector.tensor_reduce(
            total[:], e[:].rearrange("j (k c) -> j c k", c=CHUNKS), AXIS.X, ALU.add
        )
        nc.vector.tensor_sub(coef[:, AB, :], coef[:, AB, :], coef[:, A, :])
        nc.vector.tensor_sub(
            coef[:, B : A + 1, :],
            coef[:, B : A + 1, :],
            coef[:, ONE : ONE + 1, :].to_broadcast([P, 2, CHUNKS]),
        )
        nc.vector.reciprocal(total[:], total[:])
        nc.vector.tensor_sub(coef[:, AB, :], coef[:, AB, :], coef[:, B, :])
        nc.vector.tensor_mul(coef[:], coef[:], total[:].unsqueeze(1).to_broadcast([P, 4, CHUNKS]))

        spread = held.tile([P, 2, BANK], F32, name="spread")

        def spread_coefficients():
            for row, q in enumerate((A, ONE)):
                repeated = slopes.tile([P, BANK], F32, name="repeated", tag="slope")
                for c in range(PER_BANK):
                    chunk = GPSIMD_HALF * PER_BANK + c
                    nc.tensor.transpose(
                        repeated[:, c * P : (c + 1) * P],
                        coef[:, q, chunk : chunk + 1].to_broadcast([P, P]),
                        identity[:],
                    )
                nc.vector.tensor_copy(spread[:, row, :], repeated[:])

        with tc.tile_pool(name="gathered", bufs=3) as gathered:
            window, picked = [], {}
            for blk in range(BLOCKS):
                window.append(windows.tile([P, SIGNALS], F32, name="window"))
                nc.sync.dma_start(window[blk][:], x[blk * P : (blk + 1) * P, :])

            def gather(blk, side, start, count):
                if start == 0:
                    picked[blk, side] = gathered.tile([P, GATES], F32, name="picked")
                first = side * GATES + start
                nc.scalar.activation(
                    picked[blk, side][:, start : start + count],
                    window[blk][:].indirect(offsets[:, first // 16 : (first + count) // 16]),
                    ACT.Copy,
                )

            def part_of_picked(unit, side):
                blk, half = divmod(unit, HALVES)
                return picked[blk, side][:, half * BANK : (half + 1) * BANK]

            spans = [slice(c * P, (c + 1) * P) for c in range(PER_BANK)]

            def flip_a(unit):
                a = part_of_picked(unit, 0)
                a_flipped = flips.tile([P, BANK], F32, name="a_flipped", tag="flipped")
                for span in spans:
                    nc.tensor.transpose(a_flipped[:, span], a[:, span], identity[:])
                return a_flipped

            def on_gpsimd(unit):
                return unit % HALVES == GPSIMD_HALF and unit >= HALVES

            def base_on_gpsimd(unit):
                a = part_of_picked(unit, 0)
                base = work.tile([P, BANK], F32, name="base_rows")
                nc.gpsimd.tensor_tensor(base[:], a, spread[:, 0, :], ALU.mult)
                nc.gpsimd.tensor_tensor(base[:], base[:], spread[:, 1, :], ALU.add)
                return base

            def slope_and_base(unit, a_flipped):
                half = unit % HALVES
                slope_flipped = work.tile([P, BANK], F32, name="slope_flipped")
                both = not on_gpsimd(unit)
                if both:
                    base_flipped = work.tile([P, BANK], F32, name="base_flipped")
                for c, span in enumerate(spans):
                    chunk = half * PER_BANK + c
                    nc.vector.tensor_scalar(
                        slope_flipped[:, span],
                        a_flipped[:, span],
                        coef[:, AB, chunk : chunk + 1],
                        coef[:, B, chunk : chunk + 1],
                        ALU.mult,
                        ALU.add,
                    )
                    if both:
                        nc.vector.tensor_scalar(
                            base_flipped[:, span],
                            a_flipped[:, span],
                            coef[:, A, chunk : chunk + 1],
                            coef[:, ONE, chunk : chunk + 1],
                            ALU.mult,
                            ALU.add,
                        )
                return slope_flipped, base_flipped if both else None

            def flip_back(unit, slope_flipped, base_flipped):
                slope = slopes.tile([P, BANK], F32, name="slope")
                for span in spans:
                    nc.tensor.transpose(slope[:, span], slope_flipped[:, span], identity[:])
                if base_flipped is None:
                    return slope, base_on_gpsimd(unit)
                base = bases.tile([P, BANK], F32, name="base")
                for span in spans:
                    nc.tensor.transpose(base[:, span], base_flipped[:, span], identity[:])
                return slope, base

            def times_b(unit, slope, result, part):
                b = part_of_picked(unit, 1)
                nc.vector.tensor_mul(result[:, part], b[:, part], slope[:, part])

            def plus_base(unit, result, base, part):
                adder = nc.gpsimd if on_gpsimd(unit) else nc.vector
                adder.tensor_tensor(result[:, part], result[:, part], base[:, part], ALU.add)

            def store(unit, result, part):
                blk, half = divmod(unit, HALVES)
                rows = out[blk * P : (blk + 1) * P, half * BANK : (half + 1) * BANK]
                nc.sync.dma_start(rows[:, part], result[:, part])

            whole = slice(0, BANK)
            ready = {}

            def units_of(blk):
                return range(blk * HALVES, (blk + 1) * HALVES)

            def flips_of(blk):
                gather(blk, 0, 0, GATES)
                return {unit: flip_a(unit) for unit in units_of(blk)}

            def b_side(blk, pieces):
                units = units_of(blk)
                results = {unit: results_pool.tile([P, BANK], F32, name="result") for unit in units}
                for piece in range(pieces):
                    gather(blk, 1, piece * GATES // pieces, GATES // pieces)
                for unit in units:
                    times_b(unit, ready[unit][0], results[unit], whole)
                for unit in units:
                    plus_base(unit, results[unit], ready[unit][1], whole)
                for unit in reversed(units):
                    store(unit, results[unit], whole)

            def last_b_side(blk):
                for unit in units_of(blk):
                    result = results_pool.tile([P, BANK], F32, name="result")
                    for part in (slice(0, BANK // 2), slice(BANK // 2, BANK)):
                        gather(blk, 1, unit % HALVES * BANK + part.start, BANK // 2)
                        times_b(unit, ready[unit][0], result, part)
                        plus_base(unit, result, ready[unit][1], part)
                        store(unit, result, part)

            spread_coefficients()
            made = {}
            for step in range(-A_LEAD, BLOCKS):
                ahead = step + A_LEAD
                if ahead < BLOCKS:
                    flipped = flips_of(ahead)
                if step >= 0:
                    for unit in units_of(step):
                        ready[unit] = flip_back(unit, *made[unit])
                if ahead < BLOCKS:
                    for unit, a_flipped in flipped.items():
                        made[unit] = slope_and_base(unit, a_flipped)
                if 0 <= step < BLOCKS - 1:
                    b_side(step, pieces=HALVES if step == BLOCKS - 2 else 1)
            last_b_side(BLOCKS - 1)
